import numpy as np
import ml_dtypes


def mxq(x, axis, fmt="e4m3"):
    dtype, down = {"e4m3": (ml_dtypes.float8_e4m3fn, 7), "e5m2": (ml_dtypes.float8_e5m2, 14)}[fmt]
    v = np.moveaxis(np.asarray(x, np.float32).astype(ml_dtypes.bfloat16).astype(np.float64), axis, -1)
    blocks = v.reshape(v.shape[:-1] + (-1, 32))
    amax = np.abs(blocks).max(-1, keepdims=True)
    byte = np.maximum(np.where(amax > 0, np.frexp(amax)[1] - 1 + 127, 0) - down, 1)
    scale = np.exp2(byte - 127.0)
    codes = (blocks / scale).astype(np.float32).astype(dtype).astype(np.float64)
    return np.moveaxis((codes * scale).reshape(v.shape), -1, axis)


WIDE = False


def mx_kscale(k):
    if not WIDE:
        return np.ones(k)
    levels = np.array([10, -10, 5, -5, 0])
    a = np.random.permutation(np.resize(levels, k // 512 * 4)).reshape(k // 512, 4)
    idx = np.arange(k)
    return np.exp2(a[idx // 512, idx % 128 // 32])


BF16 = ml_dtypes.bfloat16


def bf(x):
    return np.asarray(x, np.float32).astype(BF16)


def f64(x):
    return np.asarray(x).astype(np.float64)


B, D, U = 256, 1024, 1024
KD = 3 * U + D


def sigmoid(v):
    return 1.0 / (1.0 + np.exp(-v))


def setup_inputs():
    s = mx_kscale(KD)

    def gate():
        return bf(np.random.standard_normal((KD, U)) * 1.25 / np.sqrt(KD) / s[:, None])

    def bias():
        return bf(np.random.standard_normal(U) * 0.5)

    return {"x": bf(np.random.standard_normal((B, D)) * s[3 * U:]),
            "left_state": bf(np.random.standard_normal((B, U)) * s[:U]),
            "top_state": bf(np.random.standard_normal((B, U)) * s[U:2 * U]),
            "diagonal_state": bf(np.random.standard_normal((B, U)) * s[2 * U:3 * U]),
            "w_rl": gate(), "b_rl": bias(), "w_rt": gate(), "b_rt": bias(), "w_rd": gate(), "b_rd": bias(),
            "u": bf(np.random.standard_normal((3 * U, U)) * 1.1 / np.sqrt(3 * U) / s[:3 * U, None]),
            "w_i": bf(np.random.standard_normal((D, U)) * 0.65 / np.sqrt(D) / s[3 * U:, None]),
            "b_i": bf(np.random.standard_normal(U) * 0.3)}


def reference(x, left_state, top_state, diagonal_state, w_rl, b_rl, w_rt, b_rt, w_rd, b_rd, u, w_i, b_i):
    states = np.concatenate([f64(left_state), f64(top_state), f64(diagonal_state)], axis=1)
    q = np.concatenate([states, f64(x)], axis=1)
    W = np.concatenate([f64(w_rl), f64(w_rt), f64(w_rd)], axis=1)
    b = np.concatenate([f64(b_rl), f64(b_rt), f64(b_rd)])
    qq = mxq(q, 1, "e4m3")
    reset = sigmoid((qq @ mxq(W, 0, "e4m3")) + b)
    xq = qq[:, 3 * U:]
    return np.tanh((xq @ mxq(f64(w_i), 0, "e4m3")) + f64(b_i)
                   + (mxq(reset * states, 1, "e4m3") @ mxq(f64(u), 0, "e4m3")))

@@ -1,0 +1,244 @@
+from contextlib import ExitStack
+
+import concourse.mybir as mybir
+from concourse.masks import make_identity
+
+F32 = mybir.dt.float32
+BF16 = mybir.dt.bfloat16
+U32 = mybir.dt.uint32
+U8 = mybir.dt.uint8
+FP8X4 = mybir.dt.float8_e4m3fn_x4
+ACT = mybir.ActivationFunctionType
+ALU = mybir.AluOpType
+
+P = 128
+PACK = 4
+K_PASS = P * PACK
+BATCH = 256
+UNITS = 1024
+FLOPS = 2 * BATCH * (4 * UNITS * 3 * UNITS + UNITS * UNITS + 3 * UNITS * UNITS)
+
+RAW_BUFS = 8
+
+
+def tile_multidimensinalgrucell_pa_kernel(
+    tc, x, left_state, top_state, diagonal_state,
+    w_rl, b_rl, w_rt, b_rt, w_rd, b_rd, u, w_i, b_i, out,
+):
+    nc = tc.nc
+    chunks = []
+    for gi, w in enumerate((w_rl, w_rt, w_rd)):
+        for c in range(8):
+            chunks.append(("gate", w, c, gi))
+    for c in range(2):
+        chunks.append(("wi", w_i, c, 0))
+    for c in range(6):
+        chunks.append(("u", u, c, 0))
+    n_chunks = len(chunks)
+
+    with ExitStack() as ctx:
+        const = ctx.enter_context(tc.tile_pool(name="const", bufs=1))
+        rawp = ctx.enter_context(tc.tile_pool(name="rawp", bufs=RAW_BUFS))
+        grpp = ctx.enter_context(tc.tile_pool(name="grpp", bufs=4))
+        codep = ctx.enter_context(tc.tile_pool(name="codep", bufs=4))
+        sigp = ctx.enter_context(tc.tile_pool(name="sigp", bufs=2))
+        outp = ctx.enter_context(tc.tile_pool(name="outp", bufs=4))
+        psum = ctx.enter_context(tc.psum_pool(name="psum", bufs=1))
+        ctx.enter_context(tc.manual_schedule())
+
+        raws = {}
+        grps = {}
+        codes = {}
+        scls = {}
+
+        def load(n):
+            w, c = chunks[n][1], chunks[n][2]
+            raw = rawp.tile([P, PACK * UNITS], BF16, name="raw")
+            nc.sync.dma_start(
+                out=raw[:],
+                in_=w[c * K_PASS:(c + 1) * K_PASS, :].rearrange("(p j) n -> p (j n)", j=PACK),
+            )
+            raws[n] = raw
+
+        def regroup(n):
+            kind = chunks[n][0]
+            grp = grpp.tile([P, PACK * UNITS], BF16, name="grp", align_bytes=64)
+            if kind == "gate":
+                src = raws[n][:].rearrange("p (j g m t) -> p g m j t", j=PACK, g=2, m=P, t=PACK)
+                dst = grp[:].rearrange("p (g t m j) -> p g m j t", g=2, t=PACK, m=P, j=PACK)
+            else:
+                src = raws[n][:].rearrange("p (j g m t) -> p g m j t", j=PACK, g=2, m=P, t=PACK)
+                dst = grp[:].rearrange("p (g m t j) -> p g m j t", g=2, m=P, t=PACK, j=PACK)
+            nc.vector.tensor_copy(out=dst[:, 0], in_=src[:, 0])
+            nc.scalar.copy(out=dst[:, 1], in_=src[:, 1])
+            grps[n] = grp
+
+        def quant(n):
+            cod = codep.tile([P, UNITS], U32, name="cod", align_bytes=64)
+            scl = codep.tile([P, UNITS], U8, name="scl", align_bytes=64)
+            for half in range(2):
+                nc.vector.quantize_mx(
+                    out=cod[:, 512 * half:512 * half + 512].bitcast(FP8X4),
+                    scales=scl[:, 512 * half:512 * half + 512],
+                    in_=grps[n][:, 2048 * half:2048 * half + 2048],
+                )
+            codes[n] = cod
+            scls[n] = scl
+
+        ident = const.tile([P, P], F32, name="ident")
+        make_identity(nc, ident[:])
+        warm = const.tile([P, 2], F32, name="warm")
+        nc.vector.memset(warm[:], 0.0)
+        bias_raw = []
+        with nc.allow_non_contiguous_dma(reason="gate biases, four neighbours to a partition"):
+            for gi, b in enumerate((b_rl, b_rt, b_rd)):
+                br = const.tile([P, 8], BF16, name="bias_raw%d" % gi)
+                nc.scalar.dma_start(
+                    out=br[:].rearrange("p (g t) -> p g t", g=2),
+                    in_=b.rearrange("(g p t) -> p g t", g=2, p=P, t=PACK),
+                )
+                bias_raw.append(br)
+        warm2 = const.tile([P, 2], F32, name="warm2")
+        nc.scalar.activation(out=warm2[:, 0:1], in_=warm[:, 0:1], func=ACT.Sigmoid)
+
+        q_raw = []
+        for i, inp in enumerate((left_state, top_state, diagonal_state, x)):
+            qr = const.tile([P, 2 * UNITS], BF16, name="q_raw%d" % i)
+            nc.sync.dma_start(
+                out=qr[:].rearrange("p (b k) -> p b k", b=2),
+                in_=inp.rearrange("(b p) k -> p b k", p=P),
+            )
+            q_raw.append(qr)
+        for n in range(RAW_BUFS):
+            load(n)
+
+        bias_f = const.tile([P, 24], F32, name="bias_f")
+        for gi in range(3):
+            nc.vector.tensor_copy(out=bias_f[:, 8 * gi:8 * gi + 8], in_=bias_raw[gi][:])
+        bias_bc = const.tile([P, UNITS], BF16, name="bias_bc")
+
+        qg = []
+        q_cod = []
+        q_scl = []
+        for c in range(8):
+            words = q_raw[c // 2][:].bitcast(F32).rearrange(
+                "p (b h w e) -> p b h e w", b=2, h=2, w=P, e=2)
+            xt = psum.tile([P, 2, BATCH], F32, name="xt%d" % c, tag="bank%d" % c)
+            for e in range(2):
+                for b in range(2):
+                    nc.tensor.transpose(xt[:, e, b * P:(b + 1) * P], words[:, b, c % 2, e, :], ident[:])
+            g = const.tile([P, PACK * BATCH], BF16, name="qg%d" % c, align_bytes=64)
+            nc.scalar.copy(
+                out=g[:].bitcast(F32).rearrange("p (b e) -> p b e", e=2),
+                in_=xt[:].rearrange("p e b -> p b e"),
+            )
+            qg.append(g)
+        for c in range(8):
+            qc = const.tile([P, BATCH], U32, name="q_cod%d" % c, align_bytes=64)
+            qs = const.tile([P, BATCH], U8, name="q_scl%d" % c, align_bytes=64)
+            nc.vector.quantize_mx(out=qc[:].bitcast(FP8X4), scales=qs[:], in_=qg[c][:])
+            q_cod.append(qc)
+            q_scl.append(qs)
+
+        rs_cod = []
+        rs_scl = []
+        acc = {}
+        sigs = {}
+
+        def mm(n):
+            kind, w, c, gi = chunks[n]
+            if kind == "gate":
+                for i in range(8):
+                    if c == 0:
+                        acc[i] = psum.tile([P, 512], F32, name="acc%d_%d" % (gi, i), tag="bank%d" % i)
+                    nc.tensor.matmul_mx(
+                        out=acc[i][:, 0:BATCH],
+                        lhsT=codes[n][:, i * P:(i + 1) * P].bitcast(FP8X4),
+                        lhsT_scale=scls[n][:, i * P:(i + 1) * P],
+                        rhs=q_cod[c][:].bitcast(FP8X4),
+                        rhs_scale=q_scl[c][:],
+                        start=(c == 0),
+                        stop=(c == 7),
+                    )
+            else:
+                first = kind == "wi" and c == 0
+                last = kind == "u" and c == 5
+                for h in range(2):
+                    for b in range(2):
+                        i = 2 * h + b
+                        if first:
+                            acc[i] = psum.tile([P, 512], F32, name="acc2_%d" % i, tag="bank%d" % i)
+                        if kind == "wi":
+                            a_cod, a_scl = q_cod[6 + c], q_scl[6 + c]
+                        else:
+                            a_cod, a_scl = rs_cod[c], rs_scl[c]
+                        nc.tensor.matmul_mx(
+                            out=acc[i][:],
+                            lhsT=a_cod[:, b * P:(b + 1) * P].bitcast(FP8X4),
+                            lhsT_scale=a_scl[:, b * P:(b + 1) * P],
+                            rhs=codes[n][:, 512 * h:512 * h + 512].bitcast(FP8X4),
+                            rhs_scale=scls[n][:, 512 * h:512 * h + 512],
+                            start=first,
+                            stop=last,
+                        )
+
+        def sigmoids(gi):
+            for g in range(2):
+                sig = sigp.tile([P, PACK * BATCH], F32, name="sig")
+                for t in range(PACK):
+                    col = 8 * gi + 4 * g + t
+                    nc.scalar.activation(
+                        out=sig[:, t * BATCH:(t + 1) * BATCH],
+                        in_=acc[4 * g + t][:, 0:BATCH],
+                        func=ACT.Sigmoid,
+                        bias=bias_f[:, col:col + 1],
+                        scale=1.0,
+                    )
+                sigs[g] = sig
+            if gi == 2:
+                nc.scalar.activation(out=warm2[:, 1:2], in_=sigs[1][:, 0:1], func=ACT.Tanh)
+
+        def products(gi):
+            for g in range(2):
+                cc = 2 * gi + g
+                rsg = sigp.tile([P, PACK * BATCH], BF16, name="rsg", align_bytes=64)
+                nc.vector.tensor_tensor(
+                    out=rsg[:].rearrange("p (b t) -> p b t", t=PACK),
+                    in0=sigs[g][:].rearrange("p (t b) -> p b t", t=PACK),
+                    in1=qg[cc][:].rearrange("p (b t) -> p b t", t=PACK),
+                    op=ALU.mult,
+                )
+                sigs[2 + g] = rsg
+            for g in range(2):
+                cc = 2 * gi + g
+                rc = const.tile([P, BATCH], U32, name="rs_cod%d" % cc, align_bytes=64)
+                rsc = const.tile([P, BATCH], U8, name="rs_scl%d" % cc, align_bytes=64)
+                nc.vector.quantize_mx(out=rc[:].bitcast(FP8X4), scales=rsc[:], in_=sigs[2 + g][:])
+                rs_cod.append(rc)
+                rs_scl.append(rsc)
+
+        for n in range(n_chunks + 1):
+            gate_done = (n - 9) // 8 if (n >= 9 and (n - 9) % 8 == 0 and n <= 25) else None
+            if gate_done is not None:
+                sigmoids(gate_done)
+            if n < n_chunks:
+                regroup(n)
+            if n + RAW_BUFS < n_chunks:
+                load(n + RAW_BUFS)
+            if n == 10:
+                nc.sync.dma_start(out=bias_bc[:], in_=b_i.partition_broadcast(P))
+            if n >= 1:
+                quant(n - 1)
+                mm(n - 1)
+            if gate_done is not None:
+                products(gate_done)
+
+        for h in range(2):
+            for b in range(2):
+                i = 2 * h + b
+                pre = outp.tile([P, 512], F32, name="pre")
+                nc.vector.tensor_tensor(
+                    out=pre[:], in0=acc[i][:], in1=bias_bc[:, 512 * h:512 * h + 512], op=ALU.add)
+                res = outp.tile([P, 512], F32, name="res")
+                nc.scalar.activation(out=res[:], in_=pre[:], func=ACT.Tanh)
+                nc.sync.dma_start(out=out[b * P:(b + 1) * P, 512 * h:512 * h + 512], in_=res[:])

@@ -19,6 +19,7 @@ UNITS = 1024
 FLOPS = 2 * BATCH * (4 * UNITS * 3 * UNITS + UNITS * UNITS + 3 * UNITS * UNITS)
 
 RAW_BUFS = 8
+V_COLS = 512
 
 
 def tile_multidimensinalgrucell_pa_kernel(
@@ -35,6 +36,7 @@ def tile_multidimensinalgrucell_pa_kernel(
     for c in range(6):
         chunks.append(("u", u, c, 0))
     n_chunks = len(chunks)
+    q_inputs = (left_state, top_state, diagonal_state, x)
 
     with ExitStack() as ctx:
         const = ctx.enter_context(tc.tile_pool(name="const", bufs=1))
@@ -50,27 +52,45 @@ def tile_multidimensinalgrucell_pa_kernel(
         grps = {}
         codes = {}
         scls = {}
+        q_raw = {}
+        qg = {}
+        q_cod = {}
+        q_scl = {}
+        rs_cod = {}
+        rs_scl = {}
+        acc = {}
+        sigs = {}
+        st = {}
+        xts = {}
 
         def load(n):
-            w, c = chunks[n][1], chunks[n][2]
+            kind, w, c = chunks[n][0], chunks[n][1], chunks[n][2]
             raw = rawp.tile([P, PACK * UNITS], BF16, name="raw")
-            nc.sync.dma_start(
-                out=raw[:],
-                in_=w[c * K_PASS:(c + 1) * K_PASS, :].rearrange("(p j) n -> p (j n)", j=PACK),
-            )
+            rows = w[c * K_PASS:(c + 1) * K_PASS, :]
+            if kind == "u":
+                nc.sync.dma_start(
+                    out=raw[:].rearrange("p (j n) -> p j n", j=PACK),
+                    in_=rows.rearrange("(j p) n -> p j n", p=P),
+                )
+            else:
+                nc.sync.dma_start(out=raw[:], in_=rows.rearrange("(p j) n -> p (j n)", j=PACK))
             raws[n] = raw
 
+        def load_q(i):
+            qr = const.tile([P, 2 * UNITS], BF16, name="q_raw%d" % i)
+            nc.sync.dma_start(
+                out=qr[:].rearrange("p (b k) -> p b k", b=2),
+                in_=q_inputs[i].rearrange("(b p) k -> p b k", p=P),
+            )
+            q_raw[i] = qr
+
         def regroup(n):
-            kind = chunks[n][0]
             grp = grpp.tile([P, PACK * UNITS], BF16, name="grp", align_bytes=64)
-            if kind == "gate":
-                src = raws[n][:].rearrange("p (j g m t) -> p g m j t", j=PACK, g=2, m=P, t=PACK)
-                dst = grp[:].rearrange("p (g t m j) -> p g m j t", g=2, t=PACK, m=P, j=PACK)
-            else:
-                src = raws[n][:].rearrange("p (j g m t) -> p g m j t", j=PACK, g=2, m=P, t=PACK)
-                dst = grp[:].rearrange("p (g m t j) -> p g m j t", g=2, m=P, t=PACK, j=PACK)
-            nc.vector.tensor_copy(out=dst[:, 0], in_=src[:, 0])
-            nc.scalar.copy(out=dst[:, 1], in_=src[:, 1])
+            src = raws[n][:].rearrange("p (j c i) -> p c j i", j=PACK, i=4)
+            dst = grp[:].rearrange("p (c i j) -> p c j i", i=4, j=PACK)
+            cut = V_COLS // 4
+            nc.vector.tensor_copy(out=dst[:, 0:cut], in_=src[:, 0:cut])
+            nc.scalar.copy(out=dst[:, cut:], in_=src[:, cut:])
             grps[n] = grp
 
         def quant(n):
@@ -85,80 +105,57 @@ def tile_multidimensinalgrucell_pa_kernel(
             codes[n] = cod
             scls[n] = scl
 
-        ident = const.tile([P, P], F32, name="ident")
-        make_identity(nc, ident[:])
-        warm = const.tile([P, 2], F32, name="warm")
-        nc.vector.memset(warm[:], 0.0)
-        bias_raw = []
-        with nc.allow_non_contiguous_dma(reason="gate biases, four neighbours to a partition"):
-            for gi, b in enumerate((b_rl, b_rt, b_rd)):
-                br = const.tile([P, 8], BF16, name="bias_raw%d" % gi)
-                nc.scalar.dma_start(
-                    out=br[:].rearrange("p (g t) -> p g t", g=2),
-                    in_=b.rearrange("(g p t) -> p g t", g=2, p=P, t=PACK),
+        def q_transposes(i):
+            for c in (2 * i, 2 * i + 1):
+                words = q_raw[i][:].bitcast(F32).rearrange(
+                    "p (b h w e) -> p b h e w", b=2, h=2, w=P, e=2)
+                xt = psum.tile([P, 2, BATCH], F32, name="xt%d" % c, tag="bank%d" % (4 + c % 4))
+                for e in range(2):
+                    for b in range(2):
+                        nc.tensor.transpose(
+                            xt[:, e, b * P:(b + 1) * P], words[:, b, c % 2, e, :], ident[:])
+                xts[c] = xt
+
+        def q_finish(i):
+            for c in (2 * i, 2 * i + 1):
+                g = const.tile([P, PACK * BATCH], BF16, name="qg%d" % c, align_bytes=64)
+                nc.scalar.copy(
+                    out=g[:].bitcast(F32).rearrange("p (b e) -> p b e", e=2),
+                    in_=xts[c][:].rearrange("p e b -> p b e"),
                 )
-                bias_raw.append(br)
-        warm2 = const.tile([P, 2], F32, name="warm2")
-        nc.scalar.activation(out=warm2[:, 0:1], in_=warm[:, 0:1], func=ACT.Sigmoid)
+                qg[c] = g
+            for c in (2 * i, 2 * i + 1):
+                qc = const.tile([P, BATCH], U32, name="q_cod%d" % c, align_bytes=64)
+                qs = const.tile([P, BATCH], U8, name="q_scl%d" % c, align_bytes=64)
+                nc.vector.quantize_mx(out=qc[:].bitcast(FP8X4), scales=qs[:], in_=qg[c][:])
+                q_cod[c] = qc
+                q_scl[c] = qs
 
-        q_raw = []
-        for i, inp in enumerate((left_state, top_state, diagonal_state, x)):
-            qr = const.tile([P, 2 * UNITS], BF16, name="q_raw%d" % i)
-            nc.sync.dma_start(
-                out=qr[:].rearrange("p (b k) -> p b k", b=2),
-                in_=inp.rearrange("(b p) k -> p b k", p=P),
-            )
-            q_raw.append(qr)
-        for n in range(RAW_BUFS):
-            load(n)
-
-        bias_f = const.tile([P, 24], F32, name="bias_f")
-        for gi in range(3):
-            nc.vector.tensor_copy(out=bias_f[:, 8 * gi:8 * gi + 8], in_=bias_raw[gi][:])
-        bias_bc = const.tile([P, UNITS], BF16, name="bias_bc")
-
-        qg = []
-        q_cod = []
-        q_scl = []
-        for c in range(8):
-            words = q_raw[c // 2][:].bitcast(F32).rearrange(
-                "p (b h w e) -> p b h e w", b=2, h=2, w=P, e=2)
-            xt = psum.tile([P, 2, BATCH], F32, name="xt%d" % c, tag="bank%d" % c)
-            for e in range(2):
-                for b in range(2):
-                    nc.tensor.transpose(xt[:, e, b * P:(b + 1) * P], words[:, b, c % 2, e, :], ident[:])
-            g = const.tile([P, PACK * BATCH], BF16, name="qg%d" % c, align_bytes=64)
-            nc.scalar.copy(
-                out=g[:].bitcast(F32).rearrange("p (b e) -> p b e", e=2),
-                in_=xt[:].rearrange("p e b -> p b e"),
-            )
-            qg.append(g)
-        for c in range(8):
-            qc = const.tile([P, BATCH], U32, name="q_cod%d" % c, align_bytes=64)
-            qs = const.tile([P, BATCH], U8, name="q_scl%d" % c, align_bytes=64)
-            nc.vector.quantize_mx(out=qc[:].bitcast(FP8X4), scales=qs[:], in_=qg[c][:])
-            q_cod.append(qc)
-            q_scl.append(qs)
-
-        rs_cod = []
-        rs_scl = []
-        acc = {}
-        sigs = {}
+        def state_t(gi):
+            for g in range(2):
+                s = psum.tile([P, PACK, BATCH], BF16, name="st%d_%d" % (gi, g), tag="bank%d" % (4 + g))
+                for t in range(PACK):
+                    for b in range(2):
+                        f0 = b * UNITS + 512 * g + P * t
+                        nc.tensor.transpose(
+                            s[:, t, b * P:(b + 1) * P], q_raw[gi][:, f0:f0 + P], ident_bf[:])
+                st[g] = s
 
         def mm(n):
             kind, w, c, gi = chunks[n]
             if kind == "gate":
                 for i in range(8):
-                    if c == 0:
-                        acc[i] = psum.tile([P, 512], F32, name="acc%d_%d" % (gi, i), tag="bank%d" % i)
+                    if c == 0 and i % 2 == 0:
+                        acc[i // 2] = psum.tile(
+                            [P, 512], F32, name="acc%d_%d" % (gi, i // 2), tag="bank%d" % (i // 2))
                     nc.tensor.matmul_mx(
-                        out=acc[i][:, 0:BATCH],
+                        out=acc[i // 2][:, (i % 2) * BATCH:(i % 2 + 1) * BATCH],
                         lhsT=codes[n][:, i * P:(i + 1) * P].bitcast(FP8X4),
                         lhsT_scale=scls[n][:, i * P:(i + 1) * P],
                         rhs=q_cod[c][:].bitcast(FP8X4),
                         rhs_scale=q_scl[c][:],
-                        start=(c == 0),
-                        stop=(c == 7),
+                        start=(c == 0 and i % 2 == 0),
+                        stop=(c == 7 and i % 2 == 1),
                     )
             else:
                 first = kind == "wi" and c == 0
@@ -186,12 +183,12 @@ def tile_multidimensinalgrucell_pa_kernel(
             for g in range(2):
                 sig = sigp.tile([P, PACK * BATCH], F32, name="sig")
                 for t in range(PACK):
-                    col = 8 * gi + 4 * g + t
+                    i = 4 * g + t
                     nc.scalar.activation(
                         out=sig[:, t * BATCH:(t + 1) * BATCH],
-                        in_=acc[4 * g + t][:, 0:BATCH],
+                        in_=acc[i // 2][:, (i % 2) * BATCH:(i % 2 + 1) * BATCH],
                         func=ACT.Sigmoid,
-                        bias=bias_f[:, col:col + 1],
+                        bias=bias_f[:, 8 * gi + i:8 * gi + i + 1],
                         scale=1.0,
                     )
                 sigs[g] = sig
@@ -200,12 +197,11 @@ def tile_multidimensinalgrucell_pa_kernel(
 
         def products(gi):
             for g in range(2):
-                cc = 2 * gi + g
                 rsg = sigp.tile([P, PACK * BATCH], BF16, name="rsg", align_bytes=64)
                 nc.vector.tensor_tensor(
                     out=rsg[:].rearrange("p (b t) -> p b t", t=PACK),
                     in0=sigs[g][:].rearrange("p (t b) -> p b t", t=PACK),
-                    in1=qg[cc][:].rearrange("p (b t) -> p b t", t=PACK),
+                    in1=st[g][:].rearrange("p t b -> p b t"),
                     op=ALU.mult,
                 )
                 sigs[2 + g] = rsg
@@ -214,8 +210,39 @@ def tile_multidimensinalgrucell_pa_kernel(
                 rc = const.tile([P, BATCH], U32, name="rs_cod%d" % cc, align_bytes=64)
                 rsc = const.tile([P, BATCH], U8, name="rs_scl%d" % cc, align_bytes=64)
                 nc.vector.quantize_mx(out=rc[:].bitcast(FP8X4), scales=rsc[:], in_=sigs[2 + g][:])
-                rs_cod.append(rc)
-                rs_scl.append(rsc)
+                rs_cod[cc] = rc
+                rs_scl[cc] = rsc
+
+        ident = const.tile([P, P], F32, name="ident")
+        make_identity(nc, ident[:])
+        ident_bf = const.tile([P, P], BF16, name="ident_bf")
+        make_identity(nc, ident_bf[:])
+        warm = const.tile([P, 2], F32, name="warm")
+        nc.vector.memset(warm[:], 0.0)
+        bias_rows = const.tile([P, P], BF16, name="bias_rows")
+        nc.vector.memset(bias_rows[:], 0.0)
+        for gi, b in enumerate((b_rl, b_rt, b_rd)):
+            nc.scalar.dma_start(
+                out=bias_rows[8 * gi:8 * gi + 8, :], in_=b.rearrange("(i m) -> i m", m=P))
+        warm2 = const.tile([P, 2], F32, name="warm2")
+        nc.scalar.activation(out=warm2[:, 0:1], in_=warm[:, 0:1], func=ACT.Sigmoid)
+
+        load(0)
+        load_q(0)
+        load(1)
+        load_q(1)
+        load(2)
+        load_q(2)
+        load(3)
+        load_q(3)
+        for n in range(4, RAW_BUFS):
+            load(n)
+
+        bias_t = psum.tile([P, P], BF16, name="bias_t", tag="bank7")
+        nc.tensor.transpose(bias_t[:], bias_rows[:], ident_bf[:])
+        bias_f = const.tile([P, 24], F32, name="bias_f")
+        nc.vector.tensor_copy(out=bias_f[:], in_=bias_t[:, 0:24])
+        bias_bc = const.tile([P, UNITS], BF16, name="bias_bc")
 
         for n in range(n_chunks + 1):
             gate_done = (n - 9) // 8 if (n >= 9 and (n - 9) % 8 == 0 and n <= 25) else None
@@ -223,6 +250,8 @@ def tile_multidimensinalgrucell_pa_kernel(
                 sigmoids(gate_done)
             if n < n_chunks:
                 regroup(n)
+            if n < 4:
+                q_transposes(n)
             if n + RAW_BUFS < n_chunks:
                 load(n + RAW_BUFS)
             if n == 10:
@@ -230,6 +259,10 @@ def tile_multidimensinalgrucell_pa_kernel(
             if n >= 1:
                 quant(n - 1)
                 mm(n - 1)
+            if n < 4:
+                q_finish(n)
+            if n in (6, 14, 22):
+                state_t((n - 6) // 8)
             if gate_done is not None:
                 products(gate_done)
 

@@ -42,7 +42,7 @@ def tile_multidimensinalgrucell_pa_kernel(
         const = ctx.enter_context(tc.tile_pool(name="const", bufs=1))
         rawp = ctx.enter_context(tc.tile_pool(name="rawp", bufs=RAW_BUFS))
         grpp = ctx.enter_context(tc.tile_pool(name="grpp", bufs=4))
-        codep = ctx.enter_context(tc.tile_pool(name="codep", bufs=4))
+        codep = ctx.enter_context(tc.tile_pool(name="codep", bufs=5))
         sigp = ctx.enter_context(tc.tile_pool(name="sigp", bufs=2))
         outp = ctx.enter_context(tc.tile_pool(name="outp", bufs=4))
         psum = ctx.enter_context(tc.psum_pool(name="psum", bufs=1))
@@ -133,7 +133,8 @@ def tile_multidimensinalgrucell_pa_kernel(
 
         def state_t(gi):
             for g in range(2):
-                s = psum.tile([P, PACK, BATCH], BF16, name="st%d_%d" % (gi, g), tag="bank%d" % (4 + g))
+                s = psum.tile(
+                    [P, PACK, BATCH], BF16, name="st%d_%d" % (gi, g), tag="bank%d" % (4 * (gi % 2) + g))
                 for t in range(PACK):
                     for b in range(2):
                         f0 = b * UNITS + 512 * g + P * t
@@ -147,7 +148,8 @@ def tile_multidimensinalgrucell_pa_kernel(
                 for i in range(8):
                     if c == 0 and i % 2 == 0:
                         acc[i // 2] = psum.tile(
-                            [P, 512], F32, name="acc%d_%d" % (gi, i // 2), tag="bank%d" % (i // 2))
+                            [P, 512], F32, name="acc%d_%d" % (gi, i // 2),
+                            tag="bank%d" % (4 * (gi % 2) + i // 2))
                     nc.tensor.matmul_mx(
                         out=acc[i // 2][:, (i % 2) * BATCH:(i % 2 + 1) * BATCH],
                         lhsT=codes[n][:, i * P:(i + 1) * P].bitcast(FP8X4),
@@ -164,7 +166,7 @@ def tile_multidimensinalgrucell_pa_kernel(
                     for b in range(2):
                         i = 2 * h + b
                         if first:
-                            acc[i] = psum.tile([P, 512], F32, name="acc2_%d" % i, tag="bank%d" % i)
+                            acc[i] = psum.tile([P, 512], F32, name="acc2_%d" % i, tag="bank%d" % (4 + i))
                         if kind == "wi":
                             a_cod, a_scl = q_cod[6 + c], q_scl[6 + c]
                         else:
@@ -222,49 +224,46 @@ def tile_multidimensinalgrucell_pa_kernel(
         bias_rows = const.tile([P, P], BF16, name="bias_rows")
         nc.vector.memset(bias_rows[:], 0.0)
         for gi, b in enumerate((b_rl, b_rt, b_rd)):
-            nc.scalar.dma_start(
+            nc.gpsimd.dma_start(
                 out=bias_rows[8 * gi:8 * gi + 8, :], in_=b.rearrange("(i m) -> i m", m=P))
         warm2 = const.tile([P, 2], F32, name="warm2")
         nc.scalar.activation(out=warm2[:, 0:1], in_=warm[:, 0:1], func=ACT.Sigmoid)
 
         load(0)
-        load_q(0)
-        load(1)
-        load_q(1)
-        load(2)
-        load_q(2)
-        load(3)
-        load_q(3)
-        for n in range(4, RAW_BUFS):
+        for i in range(4):
+            load(i + 1)
+            load_q(i)
+        for n in range(5, RAW_BUFS):
             load(n)
 
-        bias_t = psum.tile([P, P], BF16, name="bias_t", tag="bank7")
-        nc.tensor.transpose(bias_t[:], bias_rows[:], ident_bf[:])
         bias_f = const.tile([P, 24], F32, name="bias_f")
-        nc.vector.tensor_copy(out=bias_f[:], in_=bias_t[:, 0:24])
         bias_bc = const.tile([P, UNITS], BF16, name="bias_bc")
 
         for n in range(n_chunks + 1):
-            gate_done = (n - 9) // 8 if (n >= 9 and (n - 9) % 8 == 0 and n <= 25) else None
-            if gate_done is not None:
-                sigmoids(gate_done)
             if n < n_chunks:
                 regroup(n)
-            if n < 4:
-                q_transposes(n)
+            if n in (10, 18, 26):
+                sigmoids((n - 10) // 8)
+                state_t((n - 10) // 8)
+            if 1 <= n <= 4:
+                q_transposes(n - 1)
             if n + RAW_BUFS < n_chunks:
                 load(n + RAW_BUFS)
             if n == 10:
                 nc.sync.dma_start(out=bias_bc[:], in_=b_i.partition_broadcast(P))
             if n >= 1:
                 quant(n - 1)
-                mm(n - 1)
-            if n < 4:
-                q_finish(n)
-            if n in (6, 14, 22):
-                state_t((n - 6) // 8)
-            if gate_done is not None:
-                products(gate_done)
+            if 2 <= n <= 5:
+                q_finish(n - 2)
+            if n == 7:
+                bias_t = psum.tile([P, P], BF16, name="bias_t", tag="bank7")
+                nc.tensor.transpose(bias_t[:], bias_rows[:], ident_bf[:])
+                nc.vector.tensor_copy(out=bias_f[:], in_=bias_t[:, 0:24])
+            if n >= 2:
+                mm(n - 2)
+            if n in (12, 20, 28):
+                products((n - 12) // 8)
+        mm(n_chunks - 1)
 
         for h in range(2):
             for b in range(2):

@@ -19,7 +19,7 @@ UNITS = 1024
 FLOPS = 2 * BATCH * (4 * UNITS * 3 * UNITS + UNITS * UNITS + 3 * UNITS * UNITS)
 
 RAW_BUFS = 8
-V_COLS = 512
+V_COLS = 560
 
 
 def tile_multidimensinalgrucell_pa_kernel(

@@ -19,7 +19,16 @@ UNITS = 1024
 FLOPS = 2 * BATCH * (4 * UNITS * 3 * UNITS + UNITS * UNITS + 3 * UNITS * UNITS)
 
 RAW_BUFS = 8
-V_COLS = 560
+
+
+def v_cols(n):
+    if n == 0:
+        return 1024
+    if n == 31:
+        return 512
+    if 24 <= n <= 30:
+        return 424
+    return 480
 
 
 def tile_multidimensinalgrucell_pa_kernel(
@@ -88,19 +97,22 @@ def tile_multidimensinalgrucell_pa_kernel(
             grp = grpp.tile([P, PACK * UNITS], BF16, name="grp", align_bytes=64)
             src = raws[n][:].rearrange("p (j c i) -> p c j i", j=PACK, i=4)
             dst = grp[:].rearrange("p (c i j) -> p c j i", i=4, j=PACK)
-            cut = V_COLS // 4
+            cut = v_cols(n) // 4
             nc.vector.tensor_copy(out=dst[:, 0:cut], in_=src[:, 0:cut])
-            nc.scalar.copy(out=dst[:, cut:], in_=src[:, cut:])
+            if cut < UNITS // 4:
+                nc.scalar.copy(out=dst[:, cut:], in_=src[:, cut:])
             grps[n] = grp
 
         def quant(n):
             cod = codep.tile([P, UNITS], U32, name="cod", align_bytes=64)
             scl = codep.tile([P, UNITS], U8, name="scl", align_bytes=64)
-            for half in range(2):
+            pieces = 2 if n == n_chunks - 1 else 1
+            wid = UNITS // pieces
+            for h in range(pieces):
                 nc.vector.quantize_mx(
-                    out=cod[:, 512 * half:512 * half + 512].bitcast(FP8X4),
-                    scales=scl[:, 512 * half:512 * half + 512],
-                    in_=grps[n][:, 2048 * half:2048 * half + 2048],
+                    out=cod[:, wid * h:wid * (h + 1)].bitcast(FP8X4),
+                    scales=scl[:, wid * h:wid * (h + 1)],
+                    in_=grps[n][:, PACK * wid * h:PACK * wid * (h + 1)],
                 )
             codes[n] = cod
             scls[n] = scl
@@ -119,10 +131,16 @@ def tile_multidimensinalgrucell_pa_kernel(
         def q_finish(i):
             for c in (2 * i, 2 * i + 1):
                 g = const.tile([P, PACK * BATCH], BF16, name="qg%d" % c, align_bytes=64)
-                nc.scalar.copy(
-                    out=g[:].bitcast(F32).rearrange("p (b e) -> p b e", e=2),
-                    in_=xts[c][:].rearrange("p e b -> p b e"),
-                )
+                if c % 2 == 0:
+                    nc.scalar.copy(
+                        out=g[:].bitcast(F32).rearrange("p (b e) -> p b e", e=2),
+                        in_=xts[c][:].rearrange("p e b -> p b e"),
+                    )
+                else:
+                    nc.vector.tensor_copy(
+                        out=g[:].bitcast(F32).rearrange("p (b e) -> p b e", e=2),
+                        in_=xts[c][:].rearrange("p e b -> p b e"),
+                    )
                 qg[c] = g
             for c in (2 * i, 2 * i + 1):
                 qc = const.tile([P, BATCH], U32, name="q_cod%d" % c, align_bytes=64)
@@ -240,6 +258,8 @@ def tile_multidimensinalgrucell_pa_kernel(
         bias_bc = const.tile([P, UNITS], BF16, name="bias_bc")
 
         for n in range(n_chunks + 1):
+            if n == n_chunks - 1:
+                quant(n - 1)
             if n < n_chunks:
                 regroup(n)
             if n in (10, 18, 26):
@@ -251,10 +271,10 @@ def tile_multidimensinalgrucell_pa_kernel(
                 load(n + RAW_BUFS)
             if n == 10:
                 nc.sync.dma_start(out=bias_bc[:], in_=b_i.partition_broadcast(P))
-            if n >= 1:
+            if n >= 1 and n != n_chunks - 1:
                 quant(n - 1)
-            if 2 <= n <= 5:
-                q_finish(n - 2)
+            if 1 <= n <= 4:
+                q_finish(n - 1)
             if n == 7:
                 bias_t = psum.tile([P, P], BF16, name="bias_t", tag="bank7")
                 nc.tensor.transpose(bias_t[:], bias_rows[:], ident_bf[:])

@@ -19,16 +19,7 @@ UNITS = 1024
 FLOPS = 2 * BATCH * (4 * UNITS * 3 * UNITS + UNITS * UNITS + 3 * UNITS * UNITS)
 
 RAW_BUFS = 8
-
-
-def v_cols(n):
-    if n == 0:
-        return 1024
-    if n == 31:
-        return 512
-    if 24 <= n <= 30:
-        return 424
-    return 480
+V_COLS = 512
 
 
 def tile_multidimensinalgrucell_pa_kernel(
@@ -97,22 +88,19 @@ def tile_multidimensinalgrucell_pa_kernel(
             grp = grpp.tile([P, PACK * UNITS], BF16, name="grp", align_bytes=64)
             src = raws[n][:].rearrange("p (j c i) -> p c j i", j=PACK, i=4)
             dst = grp[:].rearrange("p (c i j) -> p c j i", i=4, j=PACK)
-            cut = v_cols(n) // 4
+            cut = V_COLS // 4
             nc.vector.tensor_copy(out=dst[:, 0:cut], in_=src[:, 0:cut])
-            if cut < UNITS // 4:
-                nc.scalar.copy(out=dst[:, cut:], in_=src[:, cut:])
+            nc.scalar.copy(out=dst[:, cut:], in_=src[:, cut:])
             grps[n] = grp
 
         def quant(n):
             cod = codep.tile([P, UNITS], U32, name="cod", align_bytes=64)
             scl = codep.tile([P, UNITS], U8, name="scl", align_bytes=64)
-            pieces = 2 if n == n_chunks - 1 else 1
-            wid = UNITS // pieces
-            for h in range(pieces):
+            for half in range(2):
                 nc.vector.quantize_mx(
-                    out=cod[:, wid * h:wid * (h + 1)].bitcast(FP8X4),
-                    scales=scl[:, wid * h:wid * (h + 1)],
-                    in_=grps[n][:, PACK * wid * h:PACK * wid * (h + 1)],
+                    out=cod[:, 512 * half:512 * half + 512].bitcast(FP8X4),
+                    scales=scl[:, 512 * half:512 * half + 512],
+                    in_=grps[n][:, 2048 * half:2048 * half + 2048],
                 )
             codes[n] = cod
             scls[n] = scl
@@ -131,16 +119,10 @@ def tile_multidimensinalgrucell_pa_kernel(
         def q_finish(i):
             for c in (2 * i, 2 * i + 1):
                 g = const.tile([P, PACK * BATCH], BF16, name="qg%d" % c, align_bytes=64)
-                if c % 2 == 0:
-                    nc.scalar.copy(
-                        out=g[:].bitcast(F32).rearrange("p (b e) -> p b e", e=2),
-                        in_=xts[c][:].rearrange("p e b -> p b e"),
-                    )
-                else:
-                    nc.vector.tensor_copy(
-                        out=g[:].bitcast(F32).rearrange("p (b e) -> p b e", e=2),
-                        in_=xts[c][:].rearrange("p e b -> p b e"),
-                    )
+                nc.scalar.copy(
+                    out=g[:].bitcast(F32).rearrange("p (b e) -> p b e", e=2),
+                    in_=xts[c][:].rearrange("p e b -> p b e"),
+                )
                 qg[c] = g
             for c in (2 * i, 2 * i + 1):
                 qc = const.tile([P, BATCH], U32, name="q_cod%d" % c, align_bytes=64)
@@ -258,8 +240,6 @@ def tile_multidimensinalgrucell_pa_kernel(
         bias_bc = const.tile([P, UNITS], BF16, name="bias_bc")
 
         for n in range(n_chunks + 1):
-            if n == n_chunks - 1:
-                quant(n - 1)
             if n < n_chunks:
                 regroup(n)
             if n in (10, 18, 26):
@@ -269,12 +249,12 @@ def tile_multidimensinalgrucell_pa_kernel(
                 q_transposes(n - 1)
             if n + RAW_BUFS < n_chunks:
                 load(n + RAW_BUFS)
-            if n == 10:
+            if n == 24:
                 nc.sync.dma_start(out=bias_bc[:], in_=b_i.partition_broadcast(P))
-            if n >= 1 and n != n_chunks - 1:
+            if n >= 1:
                 quant(n - 1)
-            if 1 <= n <= 4:
-                q_finish(n - 1)
+            if 2 <= n <= 5:
+                q_finish(n - 2)
             if n == 7:
                 bias_t = psum.tile([P, P], BF16, name="bias_t", tag="bank7")
                 nc.tensor.transpose(bias_t[:], bias_rows[:], ident_bf[:])

@@ -41,8 +41,8 @@ def tile_multidimensinalgrucell_pa_kernel(
     with ExitStack() as ctx:
         const = ctx.enter_context(tc.tile_pool(name="const", bufs=1))
         rawp = ctx.enter_context(tc.tile_pool(name="rawp", bufs=RAW_BUFS))
-        grpp = ctx.enter_context(tc.tile_pool(name="grpp", bufs=4))
-        codep = ctx.enter_context(tc.tile_pool(name="codep", bufs=5))
+        grpp = ctx.enter_context(tc.tile_pool(name="grpp", bufs=6))
+        codep = ctx.enter_context(tc.tile_pool(name="codep", bufs=6))
         sigp = ctx.enter_context(tc.tile_pool(name="sigp", bufs=2))
         outp = ctx.enter_context(tc.tile_pool(name="outp", bufs=4))
         psum = ctx.enter_context(tc.psum_pool(name="psum", bufs=1))
@@ -96,11 +96,13 @@ def tile_multidimensinalgrucell_pa_kernel(
         def quant(n):
             cod = codep.tile([P, UNITS], U32, name="cod", align_bytes=64)
             scl = codep.tile([P, UNITS], U8, name="scl", align_bytes=64)
-            for half in range(2):
+            pieces = 2 if n == n_chunks - 1 else 1
+            wid = UNITS // pieces
+            for h in range(pieces):
                 nc.vector.quantize_mx(
-                    out=cod[:, 512 * half:512 * half + 512].bitcast(FP8X4),
-                    scales=scl[:, 512 * half:512 * half + 512],
-                    in_=grps[n][:, 2048 * half:2048 * half + 2048],
+                    out=cod[:, wid * h:wid * (h + 1)].bitcast(FP8X4),
+                    scales=scl[:, wid * h:wid * (h + 1)],
+                    in_=grps[n][:, PACK * wid * h:PACK * wid * (h + 1)],
                 )
             codes[n] = cod
             scls[n] = scl
@@ -239,31 +241,35 @@ def tile_multidimensinalgrucell_pa_kernel(
         bias_f = const.tile([P, 24], F32, name="bias_f")
         bias_bc = const.tile([P, UNITS], BF16, name="bias_bc")
 
-        for n in range(n_chunks + 1):
-            if n < n_chunks:
+        groups = [[n] for n in range(6)] + [[n, n + 1] for n in range(6, n_chunks, 2)] + [[]]
+        for k, group in enumerate(groups):
+            before = groups[k - 1] if k >= 1 else []
+            for n in group:
                 regroup(n)
-            if n in (10, 18, 26):
-                sigmoids((n - 10) // 8)
-                state_t((n - 10) // 8)
-            if 1 <= n <= 4:
-                q_transposes(n - 1)
-            if n + RAW_BUFS < n_chunks:
-                load(n + RAW_BUFS)
-            if n == 24:
+            for gi in range(3):
+                if k == 8 + 4 * gi:
+                    sigmoids(gi)
+                    state_t(gi)
+            if 1 <= k <= 4:
+                q_transposes(k - 1)
+            for n in group:
+                if n + RAW_BUFS < n_chunks:
+                    load(n + RAW_BUFS)
+            if k == 16:
                 nc.sync.dma_start(out=bias_bc[:], in_=b_i.partition_broadcast(P))
-            if n >= 1:
-                quant(n - 1)
-            if 2 <= n <= 5:
-                q_finish(n - 2)
-            if n == 7:
+            for n in before:
+                quant(n)
+            if 1 <= k <= 4:
+                q_finish(k - 1)
+            if k == 6:
                 bias_t = psum.tile([P, P], BF16, name="bias_t", tag="bank7")
                 nc.tensor.transpose(bias_t[:], bias_rows[:], ident_bf[:])
                 nc.vector.tensor_copy(out=bias_f[:], in_=bias_t[:, 0:24])
-            if n >= 2:
-                mm(n - 2)
-            if n in (12, 20, 28):
-                products((n - 12) // 8)
-        mm(n_chunks - 1)
+            for n in before:
+                mm(n)
+            for gi in range(3):
+                if k == 9 + 4 * gi:
+                    products(gi)
 
         for h in range(2):
             for b in range(2):

@@ -19,7 +19,18 @@ UNITS = 1024
 FLOPS = 2 * BATCH * (4 * UNITS * 3 * UNITS + UNITS * UNITS + 3 * UNITS * UNITS)
 
 RAW_BUFS = 8
-V_COLS = 512
+
+
+def v_cols(n):
+    if n in (10, 18, 26):
+        return 944
+    if n in (12, 13, 20, 21, 28, 29):
+        return 200
+    if n == 31:
+        return 432
+    if 2 <= n <= 5:
+        return 560
+    return 520
 
 
 def tile_multidimensinalgrucell_pa_kernel(
@@ -41,8 +52,8 @@ def tile_multidimensinalgrucell_pa_kernel(
     with ExitStack() as ctx:
         const = ctx.enter_context(tc.tile_pool(name="const", bufs=1))
         rawp = ctx.enter_context(tc.tile_pool(name="rawp", bufs=RAW_BUFS))
-        grpp = ctx.enter_context(tc.tile_pool(name="grpp", bufs=6))
-        codep = ctx.enter_context(tc.tile_pool(name="codep", bufs=6))
+        grpp = ctx.enter_context(tc.tile_pool(name="grpp", bufs=4))
+        codep = ctx.enter_context(tc.tile_pool(name="codep", bufs=5))
         sigp = ctx.enter_context(tc.tile_pool(name="sigp", bufs=2))
         outp = ctx.enter_context(tc.tile_pool(name="outp", bufs=4))
         psum = ctx.enter_context(tc.psum_pool(name="psum", bufs=1))
@@ -88,7 +99,7 @@ def tile_multidimensinalgrucell_pa_kernel(
             grp = grpp.tile([P, PACK * UNITS], BF16, name="grp", align_bytes=64)
             src = raws[n][:].rearrange("p (j c i) -> p c j i", j=PACK, i=4)
             dst = grp[:].rearrange("p (c i j) -> p c j i", i=4, j=PACK)
-            cut = V_COLS // 4
+            cut = v_cols(n) // 4
             nc.vector.tensor_copy(out=dst[:, 0:cut], in_=src[:, 0:cut])
             nc.scalar.copy(out=dst[:, cut:], in_=src[:, cut:])
             grps[n] = grp
@@ -96,13 +107,11 @@ def tile_multidimensinalgrucell_pa_kernel(
         def quant(n):
             cod = codep.tile([P, UNITS], U32, name="cod", align_bytes=64)
             scl = codep.tile([P, UNITS], U8, name="scl", align_bytes=64)
-            pieces = 2 if n == n_chunks - 1 else 1
-            wid = UNITS // pieces
-            for h in range(pieces):
+            for half in range(2):
                 nc.vector.quantize_mx(
-                    out=cod[:, wid * h:wid * (h + 1)].bitcast(FP8X4),
-                    scales=scl[:, wid * h:wid * (h + 1)],
-                    in_=grps[n][:, PACK * wid * h:PACK * wid * (h + 1)],
+                    out=cod[:, 512 * half:512 * half + 512].bitcast(FP8X4),
+                    scales=scl[:, 512 * half:512 * half + 512],
+                    in_=grps[n][:, 2048 * half:2048 * half + 2048],
                 )
             codes[n] = cod
             scls[n] = scl
@@ -241,35 +250,31 @@ def tile_multidimensinalgrucell_pa_kernel(
         bias_f = const.tile([P, 24], F32, name="bias_f")
         bias_bc = const.tile([P, UNITS], BF16, name="bias_bc")
 
-        groups = [[n] for n in range(6)] + [[n, n + 1] for n in range(6, n_chunks, 2)] + [[]]
-        for k, group in enumerate(groups):
-            before = groups[k - 1] if k >= 1 else []
-            for n in group:
+        for n in range(n_chunks + 1):
+            if n < n_chunks:
                 regroup(n)
-            for gi in range(3):
-                if k == 8 + 4 * gi:
-                    sigmoids(gi)
-                    state_t(gi)
-            if 1 <= k <= 4:
-                q_transposes(k - 1)
-            for n in group:
-                if n + RAW_BUFS < n_chunks:
-                    load(n + RAW_BUFS)
-            if k == 16:
+            if n in (10, 18, 26):
+                sigmoids((n - 10) // 8)
+                state_t((n - 10) // 8)
+            if 1 <= n <= 4:
+                q_transposes(n - 1)
+            if n + RAW_BUFS < n_chunks:
+                load(n + RAW_BUFS)
+            if n == 24:
                 nc.sync.dma_start(out=bias_bc[:], in_=b_i.partition_broadcast(P))
-            for n in before:
-                quant(n)
-            if 1 <= k <= 4:
-                q_finish(k - 1)
-            if k == 6:
+            if n >= 1:
+                quant(n - 1)
+            if 2 <= n <= 5:
+                q_finish(n - 2)
+            if n == 7:
                 bias_t = psum.tile([P, P], BF16, name="bias_t", tag="bank7")
                 nc.tensor.transpose(bias_t[:], bias_rows[:], ident_bf[:])
                 nc.vector.tensor_copy(out=bias_f[:], in_=bias_t[:, 0:24])
-            for n in before:
-                mm(n)
-            for gi in range(3):
-                if k == 9 + 4 * gi:
-                    products(gi)
+            if n >= 2:
+                mm(n - 2)
+            if n in (12, 20, 28):
+                products((n - 12) // 8)
+        mm(n_chunks - 1)
 
         for h in range(2):
             for b in range(2):

from contextlib import ExitStack

import concourse.mybir as mybir
from concourse.masks import make_identity

F32 = mybir.dt.float32
BF16 = mybir.dt.bfloat16
U32 = mybir.dt.uint32
U8 = mybir.dt.uint8
FP8X4 = mybir.dt.float8_e4m3fn_x4
ACT = mybir.ActivationFunctionType
ALU = mybir.AluOpType

P = 128
PACK = 4
K_PASS = P * PACK
BATCH = 256
UNITS = 1024
FLOPS = 2 * BATCH * (4 * UNITS * 3 * UNITS + UNITS * UNITS + 3 * UNITS * UNITS)

RAW_BUFS = 8


def v_cols(n):
    if n in (10, 18, 26):
        return 944
    if n in (12, 13, 20, 21, 28, 29):
        return 200
    if n == 31:
        return 432
    if 2 <= n <= 5:
        return 560
    return 520


def tile_multidimensinalgrucell_pa_kernel(
    tc, x, left_state, top_state, diagonal_state,
    w_rl, b_rl, w_rt, b_rt, w_rd, b_rd, u, w_i, b_i, out,
):
    nc = tc.nc
    chunks = []
    for gi, w in enumerate((w_rl, w_rt, w_rd)):
        for c in range(8):
            chunks.append(("gate", w, c, gi))
    for c in range(2):
        chunks.append(("wi", w_i, c, 0))
    for c in range(6):
        chunks.append(("u", u, c, 0))
    n_chunks = len(chunks)
    q_inputs = (left_state, top_state, diagonal_state, x)

    with ExitStack() as ctx:
        const = ctx.enter_context(tc.tile_pool(name="const", bufs=1))
        rawp = ctx.enter_context(tc.tile_pool(name="rawp", bufs=RAW_BUFS))
        grpp = ctx.enter_context(tc.tile_pool(name="grpp", bufs=4))
        codep = ctx.enter_context(tc.tile_pool(name="codep", bufs=5))
        sigp = ctx.enter_context(tc.tile_pool(name="sigp", bufs=2))
        outp = ctx.enter_context(tc.tile_pool(name="outp", bufs=4))
        psum = ctx.enter_context(tc.psum_pool(name="psum", bufs=1))
        ctx.enter_context(tc.manual_schedule())

        raws = {}
        grps = {}
        codes = {}
        scls = {}
        q_raw = {}
        qg = {}
        q_cod = {}
        q_scl = {}
        rs_cod = {}
        rs_scl = {}
        acc = {}
        sigs = {}
        st = {}
        xts = {}

        def load(n):
            kind, w, c = chunks[n][0], chunks[n][1], chunks[n][2]
            raw = rawp.tile([P, PACK * UNITS], BF16, name="raw")
            rows = w[c * K_PASS:(c + 1) * K_PASS, :]
            if kind == "u":
                nc.sync.dma_start(
                    out=raw[:].rearrange("p (j n) -> p j n", j=PACK),
                    in_=rows.rearrange("(j p) n -> p j n", p=P),
                )
            else:
                nc.sync.dma_start(out=raw[:], in_=rows.rearrange("(p j) n -> p (j n)", j=PACK))
            raws[n] = raw

        def load_q(i):
            qr = const.tile([P, 2 * UNITS], BF16, name="q_raw%d" % i)
            nc.sync.dma_start(
                out=qr[:].rearrange("p (b k) -> p b k", b=2),
                in_=q_inputs[i].rearrange("(b p) k -> p b k", p=P),
            )
            q_raw[i] = qr

        def regroup(n):
            grp = grpp.tile([P, PACK * UNITS], BF16, name="grp", align_bytes=64)
            src = raws[n][:].rearrange("p (j c i) -> p c j i", j=PACK, i=4)
            dst = grp[:].rearrange("p (c i j) -> p c j i", i=4, j=PACK)
            cut = v_cols(n) // 4
            nc.vector.tensor_copy(out=dst[:, 0:cut], in_=src[:, 0:cut])
            nc.scalar.copy(out=dst[:, cut:], in_=src[:, cut:])
            grps[n] = grp

        def quant(n):
            cod = codep.tile([P, UNITS], U32, name="cod", align_bytes=64)
            scl = codep.tile([P, UNITS], U8, name="scl", align_bytes=64)
            for half in range(2):
                nc.vector.quantize_mx(
                    out=cod[:, 512 * half:512 * half + 512].bitcast(FP8X4),
                    scales=scl[:, 512 * half:512 * half + 512],
                    in_=grps[n][:, 2048 * half:2048 * half + 2048],
                )
            codes[n] = cod
            scls[n] = scl

        def q_transposes(i):
            for c in (2 * i, 2 * i + 1):
                words = q_raw[i][:].bitcast(F32).rearrange(
                    "p (b h w e) -> p b h e w", b=2, h=2, w=P, e=2)
                xt = psum.tile([P, 2, BATCH], F32, name="xt%d" % c, tag="bank%d" % (4 + c % 4))
                for e in range(2):
                    for b in range(2):
                        nc.tensor.transpose(
                            xt[:, e, b * P:(b + 1) * P], words[:, b, c % 2, e, :], ident[:])
                xts[c] = xt

        def q_finish(i):
            for c in (2 * i, 2 * i + 1):
                g = const.tile([P, PACK * BATCH], BF16, name="qg%d" % c, align_bytes=64)
                nc.scalar.copy(
                    out=g[:].bitcast(F32).rearrange("p (b e) -> p b e", e=2),
                    in_=xts[c][:].rearrange("p e b -> p b e"),
                )
                qg[c] = g
            for c in (2 * i, 2 * i + 1):
                qc = const.tile([P, BATCH], U32, name="q_cod%d" % c, align_bytes=64)
                qs = const.tile([P, BATCH], U8, name="q_scl%d" % c, align_bytes=64)
                nc.vector.quantize_mx(out=qc[:].bitcast(FP8X4), scales=qs[:], in_=qg[c][:])
                q_cod[c] = qc
                q_scl[c] = qs

        def state_t(gi):
            for g in range(2):
                s = psum.tile(
                    [P, PACK, BATCH], BF16, name="st%d_%d" % (gi, g), tag="bank%d" % (4 * (gi % 2) + g))
                for t in range(PACK):
                    for b in range(2):
                        f0 = b * UNITS + 512 * g + P * t
                        nc.tensor.transpose(
                            s[:, t, b * P:(b + 1) * P], q_raw[gi][:, f0:f0 + P], ident_bf[:])
                st[g] = s

        def mm(n):
            kind, w, c, gi = chunks[n]
            if kind == "gate":
                for i in range(8):
                    if c == 0 and i % 2 == 0:
                        acc[i // 2] = psum.tile(
                            [P, 512], F32, name="acc%d_%d" % (gi, i // 2),
                            tag="bank%d" % (4 * (gi % 2) + i // 2))
                    nc.tensor.matmul_mx(
                        out=acc[i // 2][:, (i % 2) * BATCH:(i % 2 + 1) * BATCH],
                        lhsT=codes[n][:, i * P:(i + 1) * P].bitcast(FP8X4),
                        lhsT_scale=scls[n][:, i * P:(i + 1) * P],
                        rhs=q_cod[c][:].bitcast(FP8X4),
                        rhs_scale=q_scl[c][:],
                        start=(c == 0 and i % 2 == 0),
                        stop=(c == 7 and i % 2 == 1),
                    )
            else:
                first = kind == "wi" and c == 0
                last = kind == "u" and c == 5
                for h in range(2):
                    for b in range(2):
                        i = 2 * h + b
                        if first:
                            acc[i] = psum.tile([P, 512], F32, name="acc2_%d" % i, tag="bank%d" % (4 + i))
                        if kind == "wi":
                            a_cod, a_scl = q_cod[6 + c], q_scl[6 + c]
                        else:
                            a_cod, a_scl = rs_cod[c], rs_scl[c]
                        nc.tensor.matmul_mx(
                            out=acc[i][:],
                            lhsT=a_cod[:, b * P:(b + 1) * P].bitcast(FP8X4),
                            lhsT_scale=a_scl[:, b * P:(b + 1) * P],
                            rhs=codes[n][:, 512 * h:512 * h + 512].bitcast(FP8X4),
                            rhs_scale=scls[n][:, 512 * h:512 * h + 512],
                            start=first,
                            stop=last,
                        )

        def sigmoids(gi):
            for g in range(2):
                sig = sigp.tile([P, PACK * BATCH], F32, name="sig")
                for t in range(PACK):
                    i = 4 * g + t
                    nc.scalar.activation(
                        out=sig[:, t * BATCH:(t + 1) * BATCH],
                        in_=acc[i // 2][:, (i % 2) * BATCH:(i % 2 + 1) * BATCH],
                        func=ACT.Sigmoid,
                        bias=bias_f[:, 8 * gi + i:8 * gi + i + 1],
                        scale=1.0,
                    )
                sigs[g] = sig
            if gi == 2:
                nc.scalar.activation(out=warm2[:, 1:2], in_=sigs[1][:, 0:1], func=ACT.Tanh)

        def products(gi):
            for g in range(2):
                rsg = sigp.tile([P, PACK * BATCH], BF16, name="rsg", align_bytes=64)
                nc.vector.tensor_tensor(
                    out=rsg[:].rearrange("p (b t) -> p b t", t=PACK),
                    in0=sigs[g][:].rearrange("p (t b) -> p b t", t=PACK),
                    in1=st[g][:].rearrange("p t b -> p b t"),
                    op=ALU.mult,
                )
                sigs[2 + g] = rsg
            for g in range(2):
                cc = 2 * gi + g
                rc = const.tile([P, BATCH], U32, name="rs_cod%d" % cc, align_bytes=64)
                rsc = const.tile([P, BATCH], U8, name="rs_scl%d" % cc, align_bytes=64)
                nc.vector.quantize_mx(out=rc[:].bitcast(FP8X4), scales=rsc[:], in_=sigs[2 + g][:])
                rs_cod[cc] = rc
                rs_scl[cc] = rsc

        ident = const.tile([P, P], F32, name="ident")
        make_identity(nc, ident[:])
        ident_bf = const.tile([P, P], BF16, name="ident_bf")
        make_identity(nc, ident_bf[:])
        warm = const.tile([P, 2], F32, name="warm")
        nc.vector.memset(warm[:], 0.0)
        bias_rows = const.tile([P, P], BF16, name="bias_rows")
        nc.vector.memset(bias_rows[:], 0.0)
        for gi, b in enumerate((b_rl, b_rt, b_rd)):
            nc.gpsimd.dma_start(
                out=bias_rows[8 * gi:8 * gi + 8, :], in_=b.rearrange("(i m) -> i m", m=P))
        warm2 = const.tile([P, 2], F32, name="warm2")
        nc.scalar.activation(out=warm2[:, 0:1], in_=warm[:, 0:1], func=ACT.Sigmoid)

        load(0)
        for i in range(4):
            load(i + 1)
            load_q(i)
        for n in range(5, RAW_BUFS):
            load(n)

        bias_f = const.tile([P, 24], F32, name="bias_f")
        bias_bc = const.tile([P, UNITS], BF16, name="bias_bc")

        for n in range(n_chunks + 1):
            if n < n_chunks:
                regroup(n)
            if n in (10, 18, 26):
                sigmoids((n - 10) // 8)
                state_t((n - 10) // 8)
            if 1 <= n <= 4:
                q_transposes(n - 1)
            if n + RAW_BUFS < n_chunks:
                load(n + RAW_BUFS)
            if n == 24:
                nc.sync.dma_start(out=bias_bc[:], in_=b_i.partition_broadcast(P))
            if n >= 1:
                quant(n - 1)
            if 2 <= n <= 5:
                q_finish(n - 2)
            if n == 7:
                bias_t = psum.tile([P, P], BF16, name="bias_t", tag="bank7")
                nc.tensor.transpose(bias_t[:], bias_rows[:], ident_bf[:])
                nc.vector.tensor_copy(out=bias_f[:], in_=bias_t[:, 0:24])
            if n >= 2:
                mm(n - 2)
            if n in (12, 20, 28):
                products((n - 12) // 8)
        mm(n_chunks - 1)

        for h in range(2):
            for b in range(2):
                i = 2 * h + b
                pre = outp.tile([P, 512], F32, name="pre")
                nc.vector.tensor_tensor(
                    out=pre[:], in0=acc[i][:], in1=bias_bc[:, 512 * h:512 * h + 512], op=ALU.add)
                res = outp.tile([P, 512], F32, name="res")
                nc.scalar.activation(out=res[:], in_=pre[:], func=ACT.Tanh)
                nc.sync.dma_start(out=out[b * P:(b + 1) * P, 512 * h:512 * h + 512], in_=res[:])
